import numpy as np
import ml_dtypes


def mxq(x, axis, fmt="e4m3"):
    dtype, down = {"e4m3": (ml_dtypes.float8_e4m3fn, 7), "e5m2": (ml_dtypes.float8_e5m2, 14)}[fmt]
    v = np.moveaxis(np.asarray(x, np.float32).astype(ml_dtypes.bfloat16).astype(np.float64), axis, -1)
    blocks = v.reshape(v.shape[:-1] + (-1, 32))
    amax = np.abs(blocks).max(-1, keepdims=True)
    byte = np.maximum(np.where(amax > 0, np.frexp(amax)[1] - 1 + 127, 0) - down, 1)
    scale = np.exp2(byte - 127.0)
    codes = (blocks / scale).astype(np.float32).astype(dtype).astype(np.float64)
    return np.moveaxis((codes * scale).reshape(v.shape), -1, axis)


WIDE = False


def mx_kscale(k):
    if not WIDE:
        return np.ones(k)
    levels = np.array([10, -10, 5, -5, 0])
    a = np.random.permutation(np.resize(levels, k // 512 * 4)).reshape(k // 512, 4)
    idx = np.arange(k)
    return np.exp2(a[idx // 512, idx % 128 // 32])


BF16 = ml_dtypes.bfloat16


def bf(x):
    return np.asarray(x, np.float32).astype(BF16)


def f64(x):
    return np.asarray(x).astype(np.float64)


B, CIN, P, COUT, W, H, HEADS = 2, 1024, 512, 2048, 16, 32, 4
D = P // HEADS
N = W * H
EPS = 1e-5


def setup_inputs():
    s = mx_kscale(P)
    rel_h = np.random.standard_normal((HEADS, D, 1, H)) * 0.25
    rel_w = np.random.standard_normal((HEADS, D, W, 1)) * 0.25
    return {
        "h1": bf(np.maximum(np.random.standard_normal((B, P, N)), 0.0) * s[None, :, None]),
        "v_w": bf(np.random.standard_normal((P, P)) * 1.5 / np.sqrt(P) / s[None, :]),
        "v_b": bf(np.random.standard_normal(P) * 0.3),
        "q": bf(np.random.standard_normal((B, P, N)) * 0.35),
        "k": bf(np.random.standard_normal((B, P, N)) * 0.35),
        "pos": bf((rel_h + rel_w).reshape(HEADS, D, N)),
        "bn2_g": bf(np.random.uniform(0.5, 1.5, P)),
        "bn2_b": bf(np.random.standard_normal(P) * 0.3),
        "bn2_m": bf(np.random.standard_normal(P) * 0.3),
        "bn2_v": bf(np.random.uniform(0.5, 1.5, P)),
    }


def reference(h1, v_w, v_b, q, k, pos, bn2_g, bn2_b, bn2_m, bn2_v):
    v = (mxq(f64(v_w), 1, "e4m3") @ mxq(f64(h1), 1, "e4m3")) + f64(v_b)[None, :, None]
    q4 = f64(q).reshape(B, HEADS, D, N)
    k4 = f64(k).reshape(B, HEADS, D, N)
    s = q4.transpose(0, 1, 3, 2) @ k4 + f64(pos).transpose(0, 2, 1) @ q4
    e = np.exp(s - s.max(-1, keepdims=True))
    o = mxq(v.reshape(B, HEADS, D, N), 3, "e4m3") @ mxq(e, 3, "e4m3").transpose(0, 1, 3, 2)
    o = (o / e.sum(-1)[:, :, None, :]).reshape(B, P, N)
    scale = f64(bn2_g) / np.sqrt(f64(bn2_v) + EPS)
    y = (o - f64(bn2_m)[None, :, None]) * scale[None, :, None] + f64(bn2_b)[None, :, None]
    return np.maximum(y, 0.0)

@@ -1,0 +1,379 @@
+from contextlib import ExitStack
+
+import concourse.masks as masks
+import concourse.mybir as mybir
+
+F32 = mybir.dt.float32
+BF16 = mybir.dt.bfloat16
+U32 = mybir.dt.uint32
+U8 = mybir.dt.uint8
+FP8X4 = mybir.dt.float8_e4m3fn_x4
+ALU = mybir.AluOpType
+ACT = mybir.ActivationFunctionType
+
+P = 128
+PACK = 4
+B = 2
+HEADS = 4
+ROUNDS = B * HEADS
+N = 512
+NT = N // P
+TILES = ROUNDS * NT
+HALVES = 2
+EPS = 1e-5
+
+FLOPS = 2 * B * N * N * N + 2 * (2 * ROUNDS * N * N * P) + 2 * ROUNDS * P * N * N
+
+
+def tile_bottleneck_transformer_pa_kernel(
+    tc, h1, v_w, v_b, q, k, pos, bn2_g, bn2_b, bn2_m, bn2_v, out
+):
+    nc = tc.nc
+    with ExitStack() as ctx:
+        consts = ctx.enter_context(tc.tile_pool(name="consts", bufs=1))
+        inputs = ctx.enter_context(tc.tile_pool(name="inputs", bufs=1))
+        operands = ctx.enter_context(tc.tile_pool(name="operands", bufs=1))
+        e_pool = ctx.enter_context(tc.tile_pool(name="e_pool", bufs=6))
+        stats = ctx.enter_context(tc.tile_pool(name="stats", bufs=3))
+        work = ctx.enter_context(tc.tile_pool(name="work", bufs=2))
+        results = ctx.enter_context(tc.tile_pool(name="results", bufs=3))
+        psum_s = ctx.enter_context(tc.psum_pool(name="psum_s", bufs=3))
+        psum_t = ctx.enter_context(tc.psum_pool(name="psum_t", bufs=2))
+        psum_1 = ctx.enter_context(tc.psum_pool(name="psum_1", bufs=1))
+        ctx.enter_context(tc.manual_schedule())
+
+        ident = consts.tile([P, P], F32, name="ident")
+        masks.make_identity(nc, ident[:])
+        ident_bf = consts.tile([P, P], BF16, name="ident_bf")
+        masks.make_identity(nc, ident_bf[:])
+        ones_bf = consts.tile([P, P], BF16, name="ones_bf")
+        nc.vector.memset(ones_bf[:], 1.0)
+
+        par_rows = consts.tile([P, P], BF16, name="par_rows")
+        nc.vector.memset(par_rows[:], 0.0)
+        for r, vec in enumerate((bn2_g, bn2_b, bn2_m, bn2_v)):
+            nc.gpsimd.dma_start(
+                out=par_rows[r * HEADS : (r + 1) * HEADS, :],
+                in_=vec.rearrange("(h d) -> h d", d=P),
+            )
+        vb_row = consts.tile([P, N], BF16, name="vb_row")
+        nc.vector.memset(vb_row[:], 0.0)
+        nc.gpsimd.dma_start(out=vb_row[0:1, :], in_=v_b.rearrange("(a o) -> a o", a=1))
+
+        q_sb = [inputs.tile([P, N], BF16, name="q_sb%d" % i) for i in range(ROUNDS)]
+        k_sb = [inputs.tile([P, N], BF16, name="k_sb%d" % i) for i in range(ROUNDS)]
+        pos_sb = [inputs.tile([P, N], BF16, name="pos_sb%d" % h) for h in range(HEADS)]
+        h_raw = [inputs.tile([P, PACK, N], BF16, name="h_raw%d" % b) for b in range(B)]
+        w_raw = inputs.tile([P, NT, N], BF16, name="w_raw")
+
+        def load_head(i):
+            b, h = divmod(i, HEADS)
+            channels = slice(h * P, (h + 1) * P)
+            nc.sync.dma_start(out=q_sb[i][:], in_=q[b, channels, :])
+            nc.sync.dma_start(out=k_sb[i][:], in_=k[b, channels, :])
+            if b == 0:
+                nc.sync.dma_start(out=pos_sb[h][:], in_=pos[h])
+
+        def load_batch(b):
+            nc.sync.dma_start(out=h_raw[b][:], in_=h1[b].rearrange("(p t) m -> p t m", t=PACK))
+
+        load_head(0)
+        load_batch(0)
+        nc.sync.dma_start(out=w_raw[:], in_=v_w.rearrange("(a o) c -> o a c", o=P))
+        for i in range(1, HEADS):
+            load_head(i)
+        load_batch(1)
+        for i in range(HEADS, ROUNDS):
+            load_head(i)
+
+        s_ps = {}
+        negmax = {}
+        esum = {}
+        e_sb = {}
+        eT_ps = {}
+        e_grouped = {}
+        e_codes = {}
+        e_scales = {}
+        vT_ps = {}
+        v_grouped = {}
+        v_codes = {}
+        v_scales = {}
+        oT_ps = {}
+        oT_sb = {}
+        o_ps = {}
+        h_codes = {}
+        h_scales = {}
+
+        def scores(g):
+            if g >= TILES:
+                return
+            i, nt = divmod(g, NT)
+            rows = slice(nt * P, (nt + 1) * P)
+            s_ps[g] = psum_s.tile([P, N], F32, name="s_ps")
+            nc.tensor.matmul(
+                out=s_ps[g][:], lhsT=q_sb[i][:, rows], rhs=k_sb[i][:], start=True, stop=False
+            )
+            nc.tensor.matmul(
+                out=s_ps[g][:],
+                lhsT=pos_sb[i % HEADS][:, rows],
+                rhs=q_sb[i][:],
+                start=False,
+                stop=True,
+            )
+
+        def rowmax(g):
+            if g >= TILES:
+                return
+            i, nt = divmod(g, NT)
+            if nt == 0:
+                negmax[i] = stats.tile([P, NT], F32, name="negmax")
+            nc.vector.reduce_max(
+                out=negmax[i][:, nt : nt + 1],
+                in_=s_ps[g][:],
+                axis=mybir.AxisListType.X,
+                negate=True,
+            )
+
+        def exponent(g):
+            if g >= TILES:
+                return
+            i, nt = divmod(g, NT)
+            if nt == 0:
+                esum[i] = stats.tile([P, NT], F32, name="esum")
+            e_sb[g] = e_pool.tile([P, N], BF16, name="e_sb")
+            nc.scalar.activation(
+                out=e_sb[g][:].rearrange("n (u p e) -> n u p e", u=2, e=2),
+                in_=s_ps[g][:].rearrange("n (u e p) -> n u p e", u=2, e=2),
+                func=ACT.Exp,
+                bias=negmax[i][:, nt : nt + 1],
+                scale=1.0,
+                accum_out=esum[i][:, nt : nt + 1],
+            )
+
+        def turn(i, half):
+            if not 0 <= i < ROUNDS:
+                return
+            eT_ps[i, half] = psum_t.tile([P, HALVES, 2, P], F32, name="eT_ps", tag="turned")
+            for l in range(HALVES):
+                words = e_sb[i * NT + half * HALVES + l][:].bitcast(F32)
+                for u in range(2):
+                    nc.tensor.transpose(
+                        eT_ps[i, half][:, l, u, :], words[:, u * P : (u + 1) * P], ident[:]
+                    )
+
+        def gather(i, half):
+            if not 0 <= i < ROUNDS:
+                return
+            if half == 0:
+                e_grouped[i] = work.tile([P, N * PACK], BF16, name="e_grouped", align_bytes=64)
+            words = e_grouped[i][:].bitcast(F32).rearrange(
+                "p (c l n u) -> p c l n u", c=HALVES, l=HALVES, u=2
+            )
+            nc.scalar.copy(
+                out=words[:, half], in_=eT_ps[i, half][:].rearrange("p l u n -> p l n u")
+            )
+
+        def quantise_e(i):
+            if not 0 <= i < ROUNDS:
+                return
+            e_codes[i] = work.tile([P, N], U32, name="e_codes", align_bytes=64)
+            e_scales[i] = work.tile([P, N], U8, name="e_scales", align_bytes=64)
+            nc.vector.quantize_mx(
+                out=e_codes[i][:].bitcast(FP8X4), scales=e_scales[i][:], in_=e_grouped[i][:]
+            )
+
+        def project(i):
+            if not 0 <= i < ROUNDS:
+                return
+            b, h = divmod(i, HEADS)
+            channels = slice(h * P, (h + 1) * P)
+            vT_ps[i] = psum_1.tile([P, PACK, P], F32, name="vT_ps", tag="vT")
+            for t in range(PACK):
+                positions = slice(t * P, (t + 1) * P)
+                nc.tensor.matmul_mx(
+                    out=vT_ps[i][:, t, :],
+                    lhsT=h_codes[b][:, positions].bitcast(FP8X4),
+                    lhsT_scale=h_scales[b][:, positions],
+                    rhs=w_codes[:, channels].bitcast(FP8X4),
+                    rhs_scale=w_scales[:, channels],
+                    start=True,
+                    stop=True,
+                )
+
+        def add_bias(i):
+            if not 0 <= i < ROUNDS:
+                return
+            h = i % HEADS
+            v_grouped[i] = work.tile([P, P, PACK], BF16, name="v_grouped", align_bytes=64)
+            nc.vector.tensor_tensor(
+                out=v_grouped[i][:],
+                in0=vT_ps[i][:].rearrange("p t d -> p d t"),
+                in1=bias_sb[:, h * P : (h + 1) * P].unsqueeze(2).to_broadcast([P, P, PACK]),
+                op=ALU.add,
+            )
+
+        def quantise_v(i):
+            if not 0 <= i < ROUNDS:
+                return
+            v_codes[i] = work.tile([P, P], U32, name="v_codes", align_bytes=64)
+            v_scales[i] = work.tile([P, P], U8, name="v_scales", align_bytes=64)
+            nc.vector.quantize_mx(
+                out=v_codes[i][:].bitcast(FP8X4),
+                scales=v_scales[i][:],
+                in_=v_grouped[i][:].rearrange("p d t -> p (d t)"),
+            )
+
+        def attend(i):
+            if not 0 <= i < ROUNDS:
+                return
+            oT_ps[i] = psum_1.tile([P, NT, P], F32, name="oT_ps", tag="oT")
+            for nt in range(NT):
+                rows = slice(nt * P, (nt + 1) * P)
+                nc.tensor.matmul_mx(
+                    out=oT_ps[i][:, nt, :],
+                    lhsT=e_codes[i][:, rows].bitcast(FP8X4),
+                    lhsT_scale=e_scales[i][:, rows],
+                    rhs=v_codes[i][:].bitcast(FP8X4),
+                    rhs_scale=v_scales[i][:],
+                    start=True,
+                    stop=True,
+                )
+
+        def normalise(i):
+            if not 0 <= i < ROUNDS:
+                return
+            rsum = stats.tile([P, NT], F32, name="rsum")
+            nc.vector.reciprocal(out=rsum[:], in_=esum[i][:])
+            oT_sb[i] = work.tile([P, NT, P], F32, name="oT_sb")
+            nc.vector.tensor_tensor(
+                out=oT_sb[i][:],
+                in0=oT_ps[i][:],
+                in1=rsum[:].unsqueeze(2).to_broadcast([P, NT, P]),
+                op=ALU.mult,
+            )
+
+        def turn_back(i):
+            if not 0 <= i < ROUNDS:
+                return
+            o_ps[i] = psum_1.tile([P, N], F32, name="o_ps", tag="o")
+            for nt in range(NT):
+                nc.tensor.transpose(
+                    o_ps[i][:, nt * P : (nt + 1) * P], oT_sb[i][:, nt, :], ident[:]
+                )
+
+        def finish(i):
+            if not 0 <= i < ROUNDS:
+                return
+            b, h = divmod(i, HEADS)
+            y_sb = results.tile([P, N], F32, name="y_sb")
+            nc.scalar.activation(
+                out=y_sb[:],
+                in_=o_ps[i][:],
+                func=ACT.Relu,
+                bias=bn_shift[:, h : h + 1],
+                scale=bn_scale[:, h : h + 1],
+            )
+            nc.sync.dma_start(out=out[b, h * P : (h + 1) * P, :], in_=y_sb[:])
+
+        def prepare_batch(b):
+            h_grouped = operands.tile([P, N, PACK], BF16, name="h_grouped%d" % b, align_bytes=64)
+            nc.vector.tensor_copy(
+                out=h_grouped[:].rearrange("p (c i) t -> p c t i", i=4),
+                in_=h_raw[b][:].rearrange("p t (c i) -> p c t i", i=4),
+            )
+            h_codes[b] = operands.tile([P, N], U32, name="h_codes%d" % b, align_bytes=64)
+            h_scales[b] = operands.tile([P, N], U8, name="h_scales%d" % b, align_bytes=64)
+            nc.vector.quantize_mx(
+                out=h_codes[b][:].bitcast(FP8X4),
+                scales=h_scales[b][:],
+                in_=h_grouped[:].rearrange("p m t -> p (m t)"),
+            )
+
+        w_grouped = operands.tile([P, N * PACK], BF16, name="w_grouped", align_bytes=64)
+        w_codes = operands.tile([P, N], U32, name="w_codes", align_bytes=64)
+        w_scales = operands.tile([P, N], U8, name="w_scales", align_bytes=64)
+
+        def turn_weights():
+            w_words = w_grouped[:].bitcast(F32).rearrange(
+                "p (c l o u) -> p c l o u", c=HALVES, l=HALVES, u=2
+            )
+            for c in range(HALVES):
+                wT_ps = psum_t.tile([P, HALVES, 2, P], F32, name="wT_ps", tag="turned")
+                for l in range(HALVES):
+                    words = (
+                        w_raw[:, c * HALVES + l, :].bitcast(F32).rearrange("o (p u) -> o u p", u=2)
+                    )
+                    for u in range(2):
+                        nc.tensor.transpose(wT_ps[:, l, u, :], words[:, u, :], ident[:])
+                nc.scalar.copy(out=w_words[:, c], in_=wT_ps[:].rearrange("p l u o -> p l o u"))
+
+        def quantise_weights():
+            nc.vector.quantize_mx(
+                out=w_codes[:].bitcast(FP8X4), scales=w_scales[:], in_=w_grouped[:]
+            )
+
+        bias_sb = consts.tile([P, N], F32, name="bias_sb")
+        bn_scale = consts.tile([P, HEADS], F32, name="bn_scale")
+        bn_shift = consts.tile([P, HEADS], F32, name="bn_shift")
+
+        def spread_small_vectors():
+            bias_ps = psum_1.tile([P, N], F32, name="bias_ps", tag="o")
+            nc.tensor.matmul(out=bias_ps[:], lhsT=ones_bf[:], rhs=vb_row[:], start=True, stop=True)
+            nc.scalar.copy(out=bias_sb[:], in_=bias_ps[:])
+            par_ps = psum_1.tile([P, P], BF16, name="par_ps", tag="oT")
+            nc.tensor.transpose(par_ps[:], par_rows[:], ident_bf[:])
+            par_sb = consts.tile([P, 4 * HEADS], F32, name="par_sb")
+            nc.scalar.copy(out=par_sb[:], in_=par_ps[:, 0 : 4 * HEADS])
+            gain = par_sb[:, 0 * HEADS : 1 * HEADS]
+            shift = par_sb[:, 1 * HEADS : 2 * HEADS]
+            mean = par_sb[:, 2 * HEADS : 3 * HEADS]
+            var = par_sb[:, 3 * HEADS : 4 * HEADS]
+            rstd = consts.tile([P, HEADS], F32, name="rstd")
+            scaled_mean = consts.tile([P, HEADS], F32, name="scaled_mean")
+            minus_half = consts.tile([P, HEADS], F32, name="minus_half")
+            nc.gpsimd.memset(minus_half[:], -0.5)
+            nc.gpsimd.tensor_scalar_add(out=rstd[:], in0=var, scalar1=EPS)
+            nc.gpsimd.tensor_tensor(out=rstd[:], in0=rstd[:], in1=minus_half[:], op=ALU.pow)
+            nc.gpsimd.tensor_tensor(out=bn_scale[:], in0=gain, in1=rstd[:], op=ALU.mult)
+            nc.gpsimd.tensor_tensor(out=scaled_mean[:], in0=mean, in1=bn_scale[:], op=ALU.mult)
+            nc.gpsimd.tensor_tensor(
+                out=bn_shift[:], in0=shift, in1=scaled_mean[:], op=ALU.subtract
+            )
+
+        scores(0)
+        scores(1)
+        rowmax(0)
+        for i in range(ROUNDS + 2):
+            g = i * NT
+            turn(i - 1, 1)
+            turn_back(i - 2)
+            scores(g + 2)
+            rowmax(g + 1)
+            if i < ROUNDS and i % HEADS == 0:
+                prepare_batch(i // HEADS)
+            exponent(g)
+            scores(g + 3)
+            gather(i - 1, 1)
+            add_bias(i - 1)
+            rowmax(g + 2)
+            exponent(g + 1)
+            if i == 0:
+                turn_weights()
+            quantise_v(i - 1)
+            quantise_e(i - 1)
+            turn(i, 0)
+            scores(g + 4)
+            finish(i - 2)
+            rowmax(g + 3)
+            if i == 0:
+                quantise_weights()
+            exponent(g + 2)
+            attend(i - 1)
+            project(i)
+            scores(g + 5)
+            gather(i, 0)
+            rowmax(g + 4)
+            exponent(g + 3)
+            normalise(i - 1)
+            if i == 0:
+                spread_small_vectors()

@@ -37,28 +37,27 @@ def tile_bottleneck_transformer_pa_kernel(
         stats = ctx.enter_context(tc.tile_pool(name="stats", bufs=3))
         work = ctx.enter_context(tc.tile_pool(name="work", bufs=2))
         results = ctx.enter_context(tc.tile_pool(name="results", bufs=3))
-        psum_s = ctx.enter_context(tc.psum_pool(name="psum_s", bufs=3))
-        psum_t = ctx.enter_context(tc.psum_pool(name="psum_t", bufs=2))
-        psum_1 = ctx.enter_context(tc.psum_pool(name="psum_1", bufs=1))
+        psum_s = ctx.enter_context(tc.psum_pool(name="psum_s", bufs=5))
+        psum_t = ctx.enter_context(tc.psum_pool(name="psum_t", bufs=1))
+        psum_o = ctx.enter_context(tc.psum_pool(name="psum_o", bufs=2))
         ctx.enter_context(tc.manual_schedule())
 
-        ident = consts.tile([P, P], F32, name="ident")
-        masks.make_identity(nc, ident[:])
-        ident_bf = consts.tile([P, P], BF16, name="ident_bf")
-        masks.make_identity(nc, ident_bf[:])
-        ones_bf = consts.tile([P, P], BF16, name="ones_bf")
-        nc.vector.memset(ones_bf[:], 1.0)
-
+        vb_row = consts.tile([P, N], BF16, name="vb_row")
+        nc.vector.memset(vb_row[:], 0.0)
         par_rows = consts.tile([P, P], BF16, name="par_rows")
         nc.vector.memset(par_rows[:], 0.0)
+        ones_bf = consts.tile([P, P], BF16, name="ones_bf")
+        nc.vector.memset(ones_bf[:], 1.0)
+        ident = consts.tile([P, P], F32, name="ident")
+        masks.make_identity(nc, ident[:])
+        nc.gpsimd.dma_start(out=vb_row[0:1, :], in_=v_b.rearrange("(a o) -> a o", a=1))
         for r, vec in enumerate((bn2_g, bn2_b, bn2_m, bn2_v)):
             nc.gpsimd.dma_start(
                 out=par_rows[r * HEADS : (r + 1) * HEADS, :],
                 in_=vec.rearrange("(h d) -> h d", d=P),
             )
-        vb_row = consts.tile([P, N], BF16, name="vb_row")
-        nc.vector.memset(vb_row[:], 0.0)
-        nc.gpsimd.dma_start(out=vb_row[0:1, :], in_=v_b.rearrange("(a o) -> a o", a=1))
+        ident_bf = consts.tile([P, P], BF16, name="ident_bf")
+        masks.make_identity(nc, ident_bf[:])
 
         q_sb = [inputs.tile([P, N], BF16, name="q_sb%d" % i) for i in range(ROUNDS)]
         k_sb = [inputs.tile([P, N], BF16, name="k_sb%d" % i) for i in range(ROUNDS)]
@@ -78,9 +77,10 @@ def tile_bottleneck_transformer_pa_kernel(
             nc.sync.dma_start(out=h_raw[b][:], in_=h1[b].rearrange("(p t) m -> p t m", t=PACK))
 
         load_head(0)
-        load_batch(0)
         nc.sync.dma_start(out=w_raw[:], in_=v_w.rearrange("(a o) c -> o a c", o=P))
-        for i in range(1, HEADS):
+        load_head(1)
+        load_batch(0)
+        for i in range(2, HEADS):
             load_head(i)
         load_batch(1)
         for i in range(HEADS, ROUNDS):
@@ -187,7 +187,7 @@ def tile_bottleneck_transformer_pa_kernel(
                 return
             b, h = divmod(i, HEADS)
             channels = slice(h * P, (h + 1) * P)
-            vT_ps[i] = psum_1.tile([P, PACK, P], F32, name="vT_ps", tag="vT")
+            vT_ps[i] = psum_o.tile([P, PACK, P], F32, name="vT_ps", tag="shared")
             for t in range(PACK):
                 positions = slice(t * P, (t + 1) * P)
                 nc.tensor.matmul_mx(
@@ -226,7 +226,7 @@ def tile_bottleneck_transformer_pa_kernel(
         def attend(i):
             if not 0 <= i < ROUNDS:
                 return
-            oT_ps[i] = psum_1.tile([P, NT, P], F32, name="oT_ps", tag="oT")
+            oT_ps[i] = psum_o.tile([P, NT, P], F32, name="oT_ps", tag="shared")
             for nt in range(NT):
                 rows = slice(nt * P, (nt + 1) * P)
                 nc.tensor.matmul_mx(
@@ -255,7 +255,7 @@ def tile_bottleneck_transformer_pa_kernel(
         def turn_back(i):
             if not 0 <= i < ROUNDS:
                 return
-            o_ps[i] = psum_1.tile([P, N], F32, name="o_ps", tag="o")
+            o_ps[i] = psum_o.tile([P, N], F32, name="o_ps", tag="shared")
             for nt in range(NT):
                 nc.tensor.transpose(
                     o_ps[i][:, nt * P : (nt + 1) * P], oT_sb[i][:, nt, :], ident[:]
@@ -293,19 +293,23 @@ def tile_bottleneck_transformer_pa_kernel(
         w_codes = operands.tile([P, N], U32, name="w_codes", align_bytes=64)
         w_scales = operands.tile([P, N], U8, name="w_scales", align_bytes=64)
 
+        wT_ps = {}
+
         def turn_weights():
-            w_words = w_grouped[:].bitcast(F32).rearrange(
-                "p (c l o u) -> p c l o u", c=HALVES, l=HALVES, u=2
-            )
             for c in range(HALVES):
-                wT_ps = psum_t.tile([P, HALVES, 2, P], F32, name="wT_ps", tag="turned")
+                wT_ps[c] = psum_o.tile([P, HALVES, 2, P], F32, name="wT_ps", tag="shared")
                 for l in range(HALVES):
                     words = (
                         w_raw[:, c * HALVES + l, :].bitcast(F32).rearrange("o (p u) -> o u p", u=2)
                     )
                     for u in range(2):
-                        nc.tensor.transpose(wT_ps[:, l, u, :], words[:, u, :], ident[:])
-                nc.scalar.copy(out=w_words[:, c], in_=wT_ps[:].rearrange("p l u o -> p l o u"))
+                        nc.tensor.transpose(wT_ps[c][:, l, u, :], words[:, u, :], ident[:])
+
+        def gather_weights(c):
+            w_words = w_grouped[:].bitcast(F32).rearrange(
+                "p (c l o u) -> p c l o u", c=HALVES, l=HALVES, u=2
+            )
+            nc.scalar.copy(out=w_words[:, c], in_=wT_ps[c][:].rearrange("p l u o -> p l o u"))
 
         def quantise_weights():
             nc.vector.quantize_mx(
@@ -317,10 +321,10 @@ def tile_bottleneck_transformer_pa_kernel(
         bn_shift = consts.tile([P, HEADS], F32, name="bn_shift")
 
         def spread_small_vectors():
-            bias_ps = psum_1.tile([P, N], F32, name="bias_ps", tag="o")
+            bias_ps = psum_o.tile([P, N], F32, name="bias_ps", tag="shared")
             nc.tensor.matmul(out=bias_ps[:], lhsT=ones_bf[:], rhs=vb_row[:], start=True, stop=True)
             nc.scalar.copy(out=bias_sb[:], in_=bias_ps[:])
-            par_ps = psum_1.tile([P, P], BF16, name="par_ps", tag="oT")
+            par_ps = psum_o.tile([P, P], BF16, name="par_ps", tag="shared")
             nc.tensor.transpose(par_ps[:], par_rows[:], ident_bf[:])
             par_sb = consts.tile([P, 4 * HEADS], F32, name="par_sb")
             nc.scalar.copy(out=par_sb[:], in_=par_ps[:, 0 : 4 * HEADS])
@@ -340,40 +344,42 @@ def tile_bottleneck_transformer_pa_kernel(
                 out=bn_shift[:], in0=shift, in1=scaled_mean[:], op=ALU.subtract
             )
 
-        scores(0)
-        scores(1)
+        for g in range(4):
+            scores(g)
+        turn_weights()
         rowmax(0)
+        rowmax(1)
         for i in range(ROUNDS + 2):
             g = i * NT
             turn(i - 1, 1)
             turn_back(i - 2)
-            scores(g + 2)
-            rowmax(g + 1)
-            if i < ROUNDS and i % HEADS == 0:
-                prepare_batch(i // HEADS)
+            scores(g + 4)
+            rowmax(g + 2)
             exponent(g)
-            scores(g + 3)
             gather(i - 1, 1)
             add_bias(i - 1)
-            rowmax(g + 2)
+            scores(g + 5)
+            rowmax(g + 3)
             exponent(g + 1)
-            if i == 0:
-                turn_weights()
+            finish(i - 2)
             quantise_v(i - 1)
             quantise_e(i - 1)
+            if i < ROUNDS and i % HEADS == 0:
+                prepare_batch(i // HEADS)
             turn(i, 0)
-            scores(g + 4)
-            finish(i - 2)
-            rowmax(g + 3)
-            if i == 0:
-                quantise_weights()
-            exponent(g + 2)
-            attend(i - 1)
-            project(i)
-            scores(g + 5)
-            gather(i, 0)
+            scores(g + 6)
             rowmax(g + 4)
-            exponent(g + 3)
-            normalise(i - 1)
+            exponent(g + 2)
+            if i == 0:
+                gather_weights(0)
+                gather_weights(1)
+                quantise_weights()
+            gather(i, 0)
+            attend(i - 1)
             if i == 0:
                 spread_small_vectors()
+            project(i)
+            scores(g + 7)
+            rowmax(g + 5)
+            exponent(g + 3)
+            normalise(i - 1)

@@ -40,7 +40,6 @@ def tile_bottleneck_transformer_pa_kernel(
         psum_s = ctx.enter_context(tc.psum_pool(name="psum_s", bufs=5))
         psum_t = ctx.enter_context(tc.psum_pool(name="psum_t", bufs=1))
         psum_o = ctx.enter_context(tc.psum_pool(name="psum_o", bufs=2))
-        ctx.enter_context(tc.manual_schedule())
 
         vb_row = consts.tile([P, N], BF16, name="vb_row")
         nc.vector.memset(vb_row[:], 0.0)

@@ -37,6 +37,7 @@ def tile_bottleneck_transformer_pa_kernel(
         stats = ctx.enter_context(tc.tile_pool(name="stats", bufs=3))
         work = ctx.enter_context(tc.tile_pool(name="work", bufs=2))
         results = ctx.enter_context(tc.tile_pool(name="results", bufs=3))
+        tail = ctx.enter_context(tc.tile_pool(name="tail", bufs=1))
         psum_s = ctx.enter_context(tc.psum_pool(name="psum_s", bufs=5))
         psum_t = ctx.enter_context(tc.psum_pool(name="psum_t", bufs=1))
         psum_o = ctx.enter_context(tc.psum_pool(name="psum_o", bufs=2))
@@ -150,7 +151,7 @@ def tile_bottleneck_transformer_pa_kernel(
             )
 
         def turn(i, half):
-            if not 0 <= i < ROUNDS:
+            if not 0 <= i < ROUNDS - 1:
                 return
             eT_ps[i, half] = psum_t.tile([P, HALVES, 2, P], F32, name="eT_ps", tag="turned")
             for l in range(HALVES):
@@ -161,7 +162,7 @@ def tile_bottleneck_transformer_pa_kernel(
                     )
 
         def gather(i, half):
-            if not 0 <= i < ROUNDS:
+            if not 0 <= i < ROUNDS - 1:
                 return
             if half == 0:
                 e_grouped[i] = work.tile([P, N * PACK], BF16, name="e_grouped", align_bytes=64)
@@ -173,7 +174,7 @@ def tile_bottleneck_transformer_pa_kernel(
             )
 
         def quantise_e(i):
-            if not 0 <= i < ROUNDS:
+            if not 0 <= i < ROUNDS - 1:
                 return
             e_codes[i] = work.tile([P, N], U32, name="e_codes", align_bytes=64)
             e_scales[i] = work.tile([P, N], U8, name="e_scales", align_bytes=64)
@@ -223,7 +224,7 @@ def tile_bottleneck_transformer_pa_kernel(
             )
 
         def attend(i):
-            if not 0 <= i < ROUNDS:
+            if not 0 <= i < ROUNDS - 1:
                 return
             oT_ps[i] = psum_o.tile([P, NT, P], F32, name="oT_ps", tag="shared")
             for nt in range(NT):
@@ -239,7 +240,7 @@ def tile_bottleneck_transformer_pa_kernel(
                 )
 
         def normalise(i):
-            if not 0 <= i < ROUNDS:
+            if not 0 <= i < ROUNDS - 1:
                 return
             rsum = stats.tile([P, NT], F32, name="rsum")
             nc.vector.reciprocal(out=rsum[:], in_=esum[i][:])
@@ -252,7 +253,7 @@ def tile_bottleneck_transformer_pa_kernel(
             )
 
         def turn_back(i):
-            if not 0 <= i < ROUNDS:
+            if not 0 <= i < ROUNDS - 1:
                 return
             o_ps[i] = psum_o.tile([P, N], F32, name="o_ps", tag="shared")
             for nt in range(NT):
@@ -261,7 +262,7 @@ def tile_bottleneck_transformer_pa_kernel(
                 )
 
         def finish(i):
-            if not 0 <= i < ROUNDS:
+            if not 0 <= i < ROUNDS - 1:
                 return
             b, h = divmod(i, HEADS)
             y_sb = results.tile([P, N], F32, name="y_sb")
@@ -343,12 +344,101 @@ def tile_bottleneck_transformer_pa_kernel(
                 out=bn_shift[:], in0=shift, in1=scaled_mean[:], op=ALU.subtract
             )
 
-        for g in range(4):
-            scores(g)
+        LAST = ROUNDS - 1
+        last_turned = {}
+        last_grouped = {}
+        last_codes = {}
+        last_scales = {}
+        last_rsum = {}
+        last_oT = {}
+        last_norm = {}
+        last_back = {}
+
+        def last_turn(tiles):
+            last_turned[tiles] = psum_s.tile([P, len(tiles), 2, P], F32, name="last_turned", tag="s_ps")
+            for l, nt in enumerate(tiles):
+                words = e_sb[LAST * NT + nt][:].bitcast(F32)
+                for u in range(2):
+                    nc.tensor.transpose(
+                        last_turned[tiles][:, l, u, :], words[:, u * P : (u + 1) * P], ident[:]
+                    )
+
+        def last_gather(tiles):
+            n = len(tiles)
+            last_grouped[tiles] = tail.tile(
+                [P, n * P * PACK], BF16, name="last_grouped%d" % tiles[0], align_bytes=64
+            )
+            nc.scalar.copy(
+                out=last_grouped[tiles][:].bitcast(F32).rearrange("p (l n u) -> p l n u", l=n, u=2),
+                in_=last_turned[tiles][:].rearrange("p l u n -> p l n u"),
+            )
+
+        def last_quantise(tiles):
+            n = len(tiles)
+            last_codes[tiles] = tail.tile([P, n * P], U32, name="last_codes%d" % tiles[0], align_bytes=64)
+            last_scales[tiles] = tail.tile([P, n * P], U8, name="last_scales%d" % tiles[0], align_bytes=64)
+            nc.vector.quantize_mx(
+                out=last_codes[tiles][:].bitcast(FP8X4),
+                scales=last_scales[tiles][:],
+                in_=last_grouped[tiles][:],
+            )
+            last_rsum[tiles] = tail.tile([P, n], F32, name="last_rsum%d" % tiles[0])
+            nc.vector.reciprocal(
+                out=last_rsum[tiles][:], in_=esum[LAST][:, tiles[0] : tiles[-1] + 1]
+            )
+
+        def last_attend(tiles):
+            last_oT[tiles] = psum_s.tile([P, len(tiles), P], F32, name="last_oT", tag="s_ps")
+            for l in range(len(tiles)):
+                rows = slice(l * P, (l + 1) * P)
+                nc.tensor.matmul_mx(
+                    out=last_oT[tiles][:, l, :],
+                    lhsT=last_codes[tiles][:, rows].bitcast(FP8X4),
+                    lhsT_scale=last_scales[tiles][:, rows],
+                    rhs=v_codes[LAST][:].bitcast(FP8X4),
+                    rhs_scale=v_scales[LAST][:],
+                    start=True,
+                    stop=True,
+                )
+
+        def last_normalise(tiles):
+            n = len(tiles)
+            last_norm[tiles] = tail.tile([P, n, P], F32, name="last_norm%d" % tiles[0])
+            nc.vector.tensor_tensor(
+                out=last_norm[tiles][:],
+                in0=last_oT[tiles][:],
+                in1=last_rsum[tiles][:].unsqueeze(2).to_broadcast([P, n, P]),
+                op=ALU.mult,
+            )
+
+        def last_turn_back(tiles):
+            last_back[tiles] = psum_s.tile([P, len(tiles) * P], F32, name="last_back", tag="s_ps")
+            for l in range(len(tiles)):
+                nc.tensor.transpose(
+                    last_back[tiles][:, l * P : (l + 1) * P], last_norm[tiles][:, l, :], ident[:]
+                )
+
+        def last_finish(tiles):
+            b, h = divmod(LAST, HEADS)
+            y_part = tail.tile([P, len(tiles) * P], F32, name="y_part%d" % tiles[0])
+            nc.scalar.activation(
+                out=y_part[:],
+                in_=last_back[tiles][:],
+                func=ACT.Relu,
+                bias=bn_shift[:, h : h + 1],
+                scale=bn_scale[:, h : h + 1],
+            )
+            nc.sync.dma_start(
+                out=out[b, h * P : (h + 1) * P, tiles[0] * P : (tiles[-1] + 1) * P], in_=y_part[:]
+            )
+
+        with tc.manual_schedule(engines={mybir.EngineType.PE}):
+            for g in range(4):
+                scores(g)
         turn_weights()
         rowmax(0)
         rowmax(1)
-        for i in range(ROUNDS + 2):
+        for i in range(ROUNDS - 1):
             g = i * NT
             turn(i - 1, 1)
             turn_back(i - 2)
@@ -382,3 +472,40 @@ def tile_bottleneck_transformer_pa_kernel(
             rowmax(g + 5)
             exponent(g + 3)
             normalise(i - 1)
+
+        first, second = (0, 1), (2, 3)
+        g = LAST * NT
+        turn(LAST - 1, 1)
+        turn_back(LAST - 2)
+        rowmax(g + 2)
+        exponent(g)
+        gather(LAST - 1, 1)
+        add_bias(LAST - 1)
+        rowmax(g + 3)
+        exponent(g + 1)
+        finish(LAST - 2)
+        quantise_v(LAST - 1)
+        quantise_e(LAST - 1)
+        project(LAST)
+        last_turn(first)
+        exponent(g + 2)
+        add_bias(LAST)
+        last_gather(first)
+        attend(LAST - 1)
+        exponent(g + 3)
+        quantise_v(LAST)
+        normalise(LAST - 1)
+        last_quantise(first)
+        last_turn(second)
+        last_gather(second)
+        last_attend(first)
+        turn_back(LAST - 1)
+        last_quantise(second)
+        last_normalise(first)
+        finish(LAST - 1)
+        last_attend(second)
+        last_turn_back(first)
+        last_normalise(second)
+        last_finish(first)
+        last_turn_back(second)
+        last_finish(second)

@@ -21,6 +21,7 @@ NT = N // P
 TILES = ROUNDS * NT
 HALVES = 2
 EPS = 1e-5
+WARM_MATMULS = 16
 
 FLOPS = 2 * B * N * N * N + 2 * (2 * ROUNDS * N * N * P) + 2 * ROUNDS * P * N * N
 
@@ -42,10 +43,12 @@ def tile_bottleneck_transformer_pa_kernel(
         psum_t = ctx.enter_context(tc.psum_pool(name="psum_t", bufs=1))
         psum_o = ctx.enter_context(tc.psum_pool(name="psum_o", bufs=2))
 
-        vb_row = consts.tile([P, N], BF16, name="vb_row")
-        nc.vector.memset(vb_row[:], 0.0)
+        zeros = consts.tile([P, P], BF16, name="zeros")
+        nc.vector.memset(zeros[:], 0.0)
         par_rows = consts.tile([P, P], BF16, name="par_rows")
         nc.vector.memset(par_rows[:], 0.0)
+        vb_row = consts.tile([P, N], BF16, name="vb_row")
+        nc.vector.memset(vb_row[:], 0.0)
         ones_bf = consts.tile([P, P], BF16, name="ones_bf")
         nc.vector.memset(ones_bf[:], 1.0)
         ident = consts.tile([P, P], F32, name="ident")
@@ -433,6 +436,11 @@ def tile_bottleneck_transformer_pa_kernel(
             )
 
         with tc.manual_schedule(engines={mybir.EngineType.PE}):
+            warm_ps = psum_o.tile([P, P], F32, name="warm_ps", tag="shared")
+            for r in range(WARM_MATMULS):
+                nc.tensor.matmul(
+                    out=warm_ps[:], lhsT=zeros[:], rhs=zeros[:], start=True, stop=True
+                )
             for g in range(4):
                 scores(g)
         turn_weights()

@@ -17,6 +17,7 @@ B = 2
 HEADS = 4
 ROUNDS = B * HEADS
 N = 512
+LAST = ROUNDS - 1
 NT = N // P
 TILES = ROUNDS * NT
 HALVES = 2
@@ -101,9 +102,11 @@ def tile_bottleneck_transformer_pa_kernel(
         v_grouped = {}
         v_codes = {}
         v_scales = {}
+        rsum = {}
         oT_ps = {}
         oT_sb = {}
         o_ps = {}
+        h_grouped = {}
         h_codes = {}
         h_scales = {}
 
@@ -242,18 +245,31 @@ def tile_bottleneck_transformer_pa_kernel(
                     stop=True,
                 )
 
+        def invert(i):
+            if not 0 <= i < LAST:
+                return
+            rsum[i] = stats.tile([P, NT], F32, name="rsum")
+            nc.vector.reciprocal(out=rsum[i][:], in_=esum[i][:])
+
         def normalise(i):
             if not 0 <= i < ROUNDS - 1:
                 return
-            rsum = stats.tile([P, NT], F32, name="rsum")
-            nc.vector.reciprocal(out=rsum[:], in_=esum[i][:])
             oT_sb[i] = work.tile([P, NT, P], F32, name="oT_sb")
-            nc.vector.tensor_tensor(
-                out=oT_sb[i][:],
-                in0=oT_ps[i][:],
-                in1=rsum[:].unsqueeze(2).to_broadcast([P, NT, P]),
-                op=ALU.mult,
-            )
+            if i == LAST - 1:
+                for nt in range(NT):
+                    nc.scalar.activation(
+                        out=oT_sb[i][:, nt, :],
+                        in_=oT_ps[i][:, nt, :],
+                        func=ACT.Copy,
+                        scale=rsum[i][:, nt : nt + 1],
+                    )
+            else:
+                nc.vector.tensor_tensor(
+                    out=oT_sb[i][:],
+                    in0=oT_ps[i][:],
+                    in1=rsum[i][:].unsqueeze(2).to_broadcast([P, NT, P]),
+                    op=ALU.mult,
+                )
 
         def turn_back(i):
             if not 0 <= i < ROUNDS - 1:
@@ -278,18 +294,30 @@ def tile_bottleneck_transformer_pa_kernel(
             )
             nc.sync.dma_start(out=out[b, h * P : (h + 1) * P, :], in_=y_sb[:])
 
+        def regroup_batch(b):
+            h_grouped[b] = operands.tile([P, N, PACK], BF16, name="h_grouped%d" % b, align_bytes=64)
+            if b == 0:
+                nc.vector.tensor_copy(
+                    out=h_grouped[b][:].rearrange("p (c i) t -> p c t i", i=4),
+                    in_=h_raw[b][:].rearrange("p t (c i) -> p c t i", i=4),
+                )
+            else:
+                nc.gpsimd.tensor_scalar(
+                    out=h_grouped[b][:],
+                    in0=h_raw[b][:].rearrange("p t m -> p m t"),
+                    scalar1=1.0,
+                    scalar2=0.0,
+                    op0=ALU.mult,
+                    op1=ALU.add,
+                )
+
         def prepare_batch(b):
-            h_grouped = operands.tile([P, N, PACK], BF16, name="h_grouped%d" % b, align_bytes=64)
-            nc.vector.tensor_copy(
-                out=h_grouped[:].rearrange("p (c i) t -> p c t i", i=4),
-                in_=h_raw[b][:].rearrange("p t (c i) -> p c t i", i=4),
-            )
             h_codes[b] = operands.tile([P, N], U32, name="h_codes%d" % b, align_bytes=64)
             h_scales[b] = operands.tile([P, N], U8, name="h_scales%d" % b, align_bytes=64)
             nc.vector.quantize_mx(
                 out=h_codes[b][:].bitcast(FP8X4),
                 scales=h_scales[b][:],
-                in_=h_grouped[:].rearrange("p m t -> p (m t)"),
+                in_=h_grouped[b][:].rearrange("p m t -> p (m t)"),
             )
 
         w_grouped = operands.tile([P, N * PACK], BF16, name="w_grouped", align_bytes=64)
@@ -347,7 +375,6 @@ def tile_bottleneck_transformer_pa_kernel(
                 out=bn_shift[:], in0=shift, in1=scaled_mean[:], op=ALU.subtract
             )
 
-        LAST = ROUNDS - 1
         last_turned = {}
         last_grouped = {}
         last_codes = {}
@@ -455,13 +482,18 @@ def tile_bottleneck_transformer_pa_kernel(
             exponent(g)
             gather(i - 1, 1)
             add_bias(i - 1)
+            invert(i - 1)
             scores(g + 5)
             rowmax(g + 3)
             exponent(g + 1)
             finish(i - 2)
             quantise_v(i - 1)
             quantise_e(i - 1)
-            if i < ROUNDS and i % HEADS == 0:
+            if i == 0:
+                regroup_batch(0)
+            if i == 1:
+                regroup_batch(1)
+            if i % HEADS == 0:
                 prepare_batch(i // HEADS)
             turn(i, 0)
             scores(g + 6)
@@ -489,6 +521,7 @@ def tile_bottleneck_transformer_pa_kernel(
         exponent(g)
         gather(LAST - 1, 1)
         add_bias(LAST - 1)
+        invert(LAST - 1)
         rowmax(g + 3)
         exponent(g + 1)
         finish(LAST - 2)
@@ -502,18 +535,18 @@ def tile_bottleneck_transformer_pa_kernel(
         attend(LAST - 1)
         exponent(g + 3)
         quantise_v(LAST)
-        normalise(LAST - 1)
         last_quantise(first)
         last_turn(second)
         last_gather(second)
+        normalise(LAST - 1)
         last_attend(first)
-        turn_back(LAST - 1)
         last_quantise(second)
         last_normalise(first)
-        finish(LAST - 1)
         last_attend(second)
+        turn_back(LAST - 1)
         last_turn_back(first)
         last_normalise(second)
+        finish(LAST - 1)
         last_finish(first)
         last_turn_back(second)
         last_finish(second)

@@ -106,7 +106,6 @@ def tile_bottleneck_transformer_pa_kernel(
         oT_ps = {}
         oT_sb = {}
         o_ps = {}
-        h_grouped = {}
         h_codes = {}
         h_scales = {}
 
@@ -294,30 +293,18 @@ def tile_bottleneck_transformer_pa_kernel(
             )
             nc.sync.dma_start(out=out[b, h * P : (h + 1) * P, :], in_=y_sb[:])
 
-        def regroup_batch(b):
-            h_grouped[b] = operands.tile([P, N, PACK], BF16, name="h_grouped%d" % b, align_bytes=64)
-            if b == 0:
-                nc.vector.tensor_copy(
-                    out=h_grouped[b][:].rearrange("p (c i) t -> p c t i", i=4),
-                    in_=h_raw[b][:].rearrange("p t (c i) -> p c t i", i=4),
-                )
-            else:
-                nc.gpsimd.tensor_scalar(
-                    out=h_grouped[b][:],
-                    in0=h_raw[b][:].rearrange("p t m -> p m t"),
-                    scalar1=1.0,
-                    scalar2=0.0,
-                    op0=ALU.mult,
-                    op1=ALU.add,
-                )
-
         def prepare_batch(b):
+            h_grouped = operands.tile([P, N, PACK], BF16, name="h_grouped%d" % b, align_bytes=64)
+            nc.vector.tensor_copy(
+                out=h_grouped[:].rearrange("p (c i) t -> p c t i", i=4),
+                in_=h_raw[b][:].rearrange("p t (c i) -> p c t i", i=4),
+            )
             h_codes[b] = operands.tile([P, N], U32, name="h_codes%d" % b, align_bytes=64)
             h_scales[b] = operands.tile([P, N], U8, name="h_scales%d" % b, align_bytes=64)
             nc.vector.quantize_mx(
                 out=h_codes[b][:].bitcast(FP8X4),
                 scales=h_scales[b][:],
-                in_=h_grouped[b][:].rearrange("p m t -> p (m t)"),
+                in_=h_grouped[:].rearrange("p m t -> p (m t)"),
             )
 
         w_grouped = operands.tile([P, N * PACK], BF16, name="w_grouped", align_bytes=64)
@@ -489,11 +476,7 @@ def tile_bottleneck_transformer_pa_kernel(
             finish(i - 2)
             quantise_v(i - 1)
             quantise_e(i - 1)
-            if i == 0:
-                regroup_batch(0)
-            if i == 1:
-                regroup_batch(1)
-            if i % HEADS == 0:
+            if i < ROUNDS and i % HEADS == 0:
                 prepare_batch(i // HEADS)
             turn(i, 0)
             scores(g + 6)

@@ -54,9 +54,8 @@ def tile_bottleneck_transformer_pa_kernel(
         nc.vector.memset(ones_bf[:], 1.0)
         ident = consts.tile([P, P], F32, name="ident")
         masks.make_identity(nc, ident[:])
-        nc.gpsimd.dma_start(out=vb_row[0:1, :], in_=v_b.rearrange("(a o) -> a o", a=1))
         for r, vec in enumerate((bn2_g, bn2_b, bn2_m, bn2_v)):
-            nc.gpsimd.dma_start(
+            nc.scalar.dma_start(
                 out=par_rows[r * HEADS : (r + 1) * HEADS, :],
                 in_=vec.rearrange("(h d) -> h d", d=P),
             )
@@ -81,6 +80,7 @@ def tile_bottleneck_transformer_pa_kernel(
             nc.sync.dma_start(out=h_raw[b][:], in_=h1[b].rearrange("(p t) m -> p t m", t=PACK))
 
         load_head(0)
+        nc.sync.dma_start(out=vb_row[0:1, :], in_=v_b.rearrange("(a o) -> a o", a=1))
         nc.sync.dma_start(out=w_raw[:], in_=v_w.rearrange("(a o) c -> o a c", o=P))
         load_head(1)
         load_batch(0)
@@ -254,21 +254,12 @@ def tile_bottleneck_transformer_pa_kernel(
             if not 0 <= i < ROUNDS - 1:
                 return
             oT_sb[i] = work.tile([P, NT, P], F32, name="oT_sb")
-            if i == LAST - 1:
-                for nt in range(NT):
-                    nc.scalar.activation(
-                        out=oT_sb[i][:, nt, :],
-                        in_=oT_ps[i][:, nt, :],
-                        func=ACT.Copy,
-                        scale=rsum[i][:, nt : nt + 1],
-                    )
-            else:
-                nc.vector.tensor_tensor(
-                    out=oT_sb[i][:],
-                    in0=oT_ps[i][:],
-                    in1=rsum[i][:].unsqueeze(2).to_broadcast([P, NT, P]),
-                    op=ALU.mult,
-                )
+            nc.vector.tensor_tensor(
+                out=oT_sb[i][:],
+                in0=oT_ps[i][:],
+                in1=rsum[i][:].unsqueeze(2).to_broadcast([P, NT, P]),
+                op=ALU.mult,
+            )
 
         def turn_back(i):
             if not 0 <= i < ROUNDS - 1:
@@ -293,19 +284,44 @@ def tile_bottleneck_transformer_pa_kernel(
             )
             nc.sync.dma_start(out=out[b, h * P : (h + 1) * P, :], in_=y_sb[:])
 
-        def prepare_batch(b):
-            h_grouped = operands.tile([P, N, PACK], BF16, name="h_grouped%d" % b, align_bytes=64)
-            nc.vector.tensor_copy(
-                out=h_grouped[:].rearrange("p (c i) t -> p c t i", i=4),
-                in_=h_raw[b][:].rearrange("p t (c i) -> p c t i", i=4),
-            )
+        h_grouped = {}
+        for b in range(B):
+            h_grouped[b] = operands.tile([P, N, PACK], BF16, name="h_grouped%d" % b, align_bytes=64)
             h_codes[b] = operands.tile([P, N], U32, name="h_codes%d" % b, align_bytes=64)
             h_scales[b] = operands.tile([P, N], U8, name="h_scales%d" % b, align_bytes=64)
+
+        def regroup(b, c):
+            positions = slice(c * P, (c + 1) * P)
+            grouped = h_grouped[b][:, positions, :].rearrange("p (c i) t -> p c t i", i=4)
+            raw = h_raw[b][:, :, positions].rearrange("p t (c i) -> p c t i", i=4)
+            if b == 1 and c < HALVES:
+                nc.scalar.copy(out=grouped, in_=raw)
+            else:
+                nc.vector.tensor_copy(out=grouped, in_=raw)
+
+        def quantise_h(b, c):
+            positions = slice(c * P, (c + 1) * P)
             nc.vector.quantize_mx(
-                out=h_codes[b][:].bitcast(FP8X4),
-                scales=h_scales[b][:],
-                in_=h_grouped[:].rearrange("p m t -> p (m t)"),
+                out=h_codes[b][:, positions].bitcast(FP8X4),
+                scales=h_scales[b][:, positions],
+                in_=h_grouped[b][:, positions, :].rearrange("p m t -> p (m t)"),
             )
+
+        def prepare(i, step):
+            if i == 0:
+                if step >= 2:
+                    regroup(0, HALVES * (step - 2))
+                    regroup(0, HALVES * (step - 2) + 1)
+                return
+            if i == 1 and step == 0:
+                for c in range(PACK):
+                    quantise_h(0, c)
+            unit = (i - 1) * NT + step - 1
+            if 0 <= unit < 2 * PACK:
+                if unit % 2 == 0:
+                    regroup(1, unit // 2)
+                else:
+                    quantise_h(1, unit // 2)
 
         w_grouped = operands.tile([P, N * PACK], BF16, name="w_grouped", align_bytes=64)
         w_codes = operands.tile([P, N], U32, name="w_codes", align_bytes=64)
@@ -338,10 +354,12 @@ def tile_bottleneck_transformer_pa_kernel(
         bn_scale = consts.tile([P, HEADS], F32, name="bn_scale")
         bn_shift = consts.tile([P, HEADS], F32, name="bn_shift")
 
-        def spread_small_vectors():
+        def spread_bias():
             bias_ps = psum_o.tile([P, N], F32, name="bias_ps", tag="shared")
             nc.tensor.matmul(out=bias_ps[:], lhsT=ones_bf[:], rhs=vb_row[:], start=True, stop=True)
             nc.scalar.copy(out=bias_sb[:], in_=bias_ps[:])
+
+        def spread_small_vectors():
             par_ps = psum_o.tile([P, P], BF16, name="par_ps", tag="shared")
             nc.tensor.transpose(par_ps[:], par_rows[:], ident_bf[:])
             par_sb = consts.tile([P, 4 * HEADS], F32, name="par_sb")
@@ -449,87 +467,101 @@ def tile_bottleneck_transformer_pa_kernel(
                 out=out[b, h * P : (h + 1) * P, tiles[0] * P : (tiles[-1] + 1) * P], in_=y_part[:]
             )
 
-        with tc.manual_schedule(engines={mybir.EngineType.PE}):
-            warm_ps = psum_o.tile([P, P], F32, name="warm_ps", tag="shared")
-            for r in range(WARM_MATMULS):
-                nc.tensor.matmul(
-                    out=warm_ps[:], lhsT=zeros[:], rhs=zeros[:], start=True, stop=True
-                )
-            for g in range(4):
-                scores(g)
-        turn_weights()
+        ctx.enter_context(
+            tc.manual_schedule(
+                engines={
+                    mybir.EngineType.PE,
+                    mybir.EngineType.DVE,
+                    mybir.EngineType.Activation,
+                }
+            )
+        )
+        warm_ps = psum_o.tile([P, P], F32, name="warm_ps", tag="shared")
+        for r in range(WARM_MATMULS):
+            nc.tensor.matmul(out=warm_ps[:], lhsT=zeros[:], rhs=zeros[:], start=True, stop=True)
+        scores(0)
+        scores(1)
+        spread_bias()
+        scores(2)
+        scores(3)
         rowmax(0)
         rowmax(1)
-        for i in range(ROUNDS - 1):
+        for i in range(LAST):
             g = i * NT
-            turn(i - 1, 1)
-            turn_back(i - 2)
             scores(g + 4)
             rowmax(g + 2)
             exponent(g)
-            gather(i - 1, 1)
-            add_bias(i - 1)
-            invert(i - 1)
+            if i == 0:
+                spread_small_vectors()
+                turn_weights()
+            normalise(i - 2)
+            turn(i - 1, 1)
+            prepare(i, 0)
+            project(i - 1)
             scores(g + 5)
             rowmax(g + 3)
             exponent(g + 1)
-            finish(i - 2)
-            quantise_v(i - 1)
-            quantise_e(i - 1)
-            if i < ROUNDS and i % HEADS == 0:
-                prepare_batch(i // HEADS)
-            turn(i, 0)
-            scores(g + 6)
-            rowmax(g + 4)
-            exponent(g + 2)
+            turn_back(i - 2)
+            gather(i - 1, 1)
             if i == 0:
                 gather_weights(0)
                 gather_weights(1)
-                quantise_weights()
-            gather(i, 0)
-            attend(i - 1)
-            if i == 0:
-                spread_small_vectors()
-            project(i)
+            add_bias(i - 1)
+            prepare(i, 1)
+            scores(g + 6)
+            rowmax(g + 4)
+            turn(i, 0)
+            exponent(g + 2)
+            invert(i - 1)
+            quantise_e(i - 1)
+            quantise_v(i - 1)
+            finish(i - 2)
+            prepare(i, 2)
             scores(g + 7)
             rowmax(g + 5)
             exponent(g + 3)
-            normalise(i - 1)
+            gather(i, 0)
+            if i == 0:
+                quantise_weights()
+            attend(i - 1)
+            prepare(i, 3)
 
         first, second = (0, 1), (2, 3)
         g = LAST * NT
-        turn(LAST - 1, 1)
-        turn_back(LAST - 2)
         rowmax(g + 2)
         exponent(g)
-        gather(LAST - 1, 1)
-        add_bias(LAST - 1)
-        invert(LAST - 1)
+        normalise(LAST - 2)
+        turn(LAST - 1, 1)
+        project(LAST - 1)
         rowmax(g + 3)
         exponent(g + 1)
-        finish(LAST - 2)
-        quantise_v(LAST - 1)
-        quantise_e(LAST - 1)
+        turn_back(LAST - 2)
+        gather(LAST - 1, 1)
+        add_bias(LAST - 1)
         project(LAST)
         last_turn(first)
         exponent(g + 2)
-        add_bias(LAST)
+        invert(LAST - 1)
+        quantise_e(LAST - 1)
+        quantise_v(LAST - 1)
+        finish(LAST - 2)
+        exponent(g + 3)
         last_gather(first)
         attend(LAST - 1)
-        exponent(g + 3)
+        add_bias(LAST)
         quantise_v(LAST)
+        normalise(LAST - 1)
         last_quantise(first)
         last_turn(second)
         last_gather(second)
-        normalise(LAST - 1)
+        turn_back(LAST - 1)
         last_attend(first)
         last_quantise(second)
         last_normalise(first)
-        last_attend(second)
-        turn_back(LAST - 1)
-        last_turn_back(first)
-        last_normalise(second)
         finish(LAST - 1)
+        last_attend(second)
+        last_normalise(second)
+        last_turn_back(first)
         last_finish(first)
         last_turn_back(second)
         last_finish(second)

@@ -93,6 +93,7 @@ def tile_bottleneck_transformer_pa_kernel(
         s_ps = {}
         negmax = {}
         esum = {}
+        esum_pair = {}
         e_sb = {}
         eT_ps = {}
         e_grouped = {}
@@ -143,8 +144,11 @@ def tile_bottleneck_transformer_pa_kernel(
             if g >= TILES:
                 return
             i, nt = divmod(g, NT)
-            if nt == 0:
-                esum[i] = stats.tile([P, NT], F32, name="esum")
+            if nt == 0 and i % 2 == 0:
+                sums = stats.tile([P, 2 * NT], F32, name="sums")
+                esum[i] = sums[:, 0:NT]
+                esum[i + 1] = sums[:, NT : 2 * NT]
+                esum_pair[i] = sums
             e_sb[g] = e_pool.tile([P, N], BF16, name="e_sb")
             nc.scalar.activation(
                 out=e_sb[g][:].rearrange("n (u p e) -> n u p e", u=2, e=2),
@@ -244,22 +248,38 @@ def tile_bottleneck_transformer_pa_kernel(
                     stop=True,
                 )
 
-        def invert(i):
-            if not 0 <= i < LAST:
+        def invert_pair(i):
+            if not (i % 2 == 0 and 0 <= i < LAST - 1):
                 return
-            rsum[i] = stats.tile([P, NT], F32, name="rsum")
-            nc.vector.reciprocal(out=rsum[i][:], in_=esum[i][:])
+            inverse = stats.tile([P, 2 * NT], F32, name="inverse")
+            nc.vector.reciprocal(out=inverse[:], in_=esum_pair[i][:])
+            rsum[i] = inverse[:, 0:NT]
+            rsum[i + 1] = inverse[:, NT : 2 * NT]
+
+        def invert(i):
+            inverse_one = stats.tile([P, NT], F32, name="inverse_one")
+            nc.vector.reciprocal(out=inverse_one[:], in_=esum[i])
+            rsum[i] = inverse_one[:]
 
         def normalise(i):
-            if not 0 <= i < ROUNDS - 1:
+            if not 0 <= i < LAST:
                 return
             oT_sb[i] = work.tile([P, NT, P], F32, name="oT_sb")
-            nc.vector.tensor_tensor(
-                out=oT_sb[i][:],
-                in0=oT_ps[i][:],
-                in1=rsum[i][:].unsqueeze(2).to_broadcast([P, NT, P]),
-                op=ALU.mult,
-            )
+            if i < 2:
+                for nt in range(NT):
+                    nc.scalar.activation(
+                        out=oT_sb[i][:, nt, :],
+                        in_=oT_ps[i][:, nt, :],
+                        func=ACT.Copy,
+                        scale=rsum[i][:, nt : nt + 1],
+                    )
+            else:
+                nc.vector.tensor_tensor(
+                    out=oT_sb[i][:],
+                    in0=oT_ps[i][:],
+                    in1=rsum[i].unsqueeze(2).to_broadcast([P, NT, P]),
+                    op=ALU.mult,
+                )
 
         def turn_back(i):
             if not 0 <= i < ROUNDS - 1:
@@ -291,37 +311,26 @@ def tile_bottleneck_transformer_pa_kernel(
             h_scales[b] = operands.tile([P, N], U8, name="h_scales%d" % b, align_bytes=64)
 
         def regroup(b, c):
-            positions = slice(c * P, (c + 1) * P)
-            grouped = h_grouped[b][:, positions, :].rearrange("p (c i) t -> p c t i", i=4)
-            raw = h_raw[b][:, :, positions].rearrange("p t (c i) -> p c t i", i=4)
-            if b == 1 and c < HALVES:
-                nc.scalar.copy(out=grouped, in_=raw)
-            else:
-                nc.vector.tensor_copy(out=grouped, in_=raw)
+            positions = slice(c * N // HALVES, (c + 1) * N // HALVES)
+            nc.vector.tensor_copy(
+                out=h_grouped[b][:, positions, :].rearrange("p (c i) t -> p c t i", i=4),
+                in_=h_raw[b][:, :, positions].rearrange("p t (c i) -> p c t i", i=4),
+            )
 
-        def quantise_h(b, c):
-            positions = slice(c * P, (c + 1) * P)
+        def quantise_h(b):
             nc.vector.quantize_mx(
-                out=h_codes[b][:, positions].bitcast(FP8X4),
-                scales=h_scales[b][:, positions],
-                in_=h_grouped[b][:, positions, :].rearrange("p m t -> p (m t)"),
+                out=h_codes[b][:].bitcast(FP8X4),
+                scales=h_scales[b][:],
+                in_=h_grouped[b][:].rearrange("p m t -> p (m t)"),
             )
 
         def prepare(i, step):
-            if i == 0:
-                if step >= 2:
-                    regroup(0, HALVES * (step - 2))
-                    regroup(0, HALVES * (step - 2) + 1)
-                return
-            if i == 1 and step == 0:
-                for c in range(PACK):
-                    quantise_h(0, c)
-            unit = (i - 1) * NT + step - 1
-            if 0 <= unit < 2 * PACK:
-                if unit % 2 == 0:
-                    regroup(1, unit // 2)
-                else:
-                    quantise_h(1, unit // 2)
+            if (i, step) in ((0, 2), (2, 1)):
+                regroup(i // 2, 0)
+            if (i, step) in ((0, 3), (2, 3)):
+                regroup(i // 2, 1)
+            if (i, step) in ((1, 0), (3, 1)):
+                quantise_h(i // 2)
 
         w_grouped = operands.tile([P, N * PACK], BF16, name="w_grouped", align_bytes=64)
         w_codes = operands.tile([P, N], U32, name="w_codes", align_bytes=64)
@@ -385,9 +394,10 @@ def tile_bottleneck_transformer_pa_kernel(
         last_codes = {}
         last_scales = {}
         last_rsum = {}
-        last_oT = {}
-        last_norm = {}
-        last_back = {}
+        last_spread_ps = {}
+        last_gain = {}
+        last_o = {}
+        last_z = {}
 
         def last_turn(tiles):
             last_turned[tiles] = psum_s.tile([P, len(tiles), 2, P], F32, name="last_turned", tag="s_ps")
@@ -417,51 +427,61 @@ def tile_bottleneck_transformer_pa_kernel(
                 scales=last_scales[tiles][:],
                 in_=last_grouped[tiles][:],
             )
-            last_rsum[tiles] = tail.tile([P, n], F32, name="last_rsum%d" % tiles[0])
+
+        def last_invert(tiles):
+            last_rsum[tiles] = tail.tile([P, len(tiles)], F32, name="last_rsum%d" % tiles[0])
             nc.vector.reciprocal(
                 out=last_rsum[tiles][:], in_=esum[LAST][:, tiles[0] : tiles[-1] + 1]
             )
 
-        def last_attend(tiles):
-            last_oT[tiles] = psum_s.tile([P, len(tiles), P], F32, name="last_oT", tag="s_ps")
-            for l in range(len(tiles)):
-                rows = slice(l * P, (l + 1) * P)
-                nc.tensor.matmul_mx(
-                    out=last_oT[tiles][:, l, :],
-                    lhsT=last_codes[tiles][:, rows].bitcast(FP8X4),
-                    lhsT_scale=last_scales[tiles][:, rows],
-                    rhs=v_codes[LAST][:].bitcast(FP8X4),
-                    rhs_scale=v_scales[LAST][:],
-                    start=True,
-                    stop=True,
-                )
-
-        def last_normalise(tiles):
-            n = len(tiles)
-            last_norm[tiles] = tail.tile([P, n, P], F32, name="last_norm%d" % tiles[0])
-            nc.vector.tensor_tensor(
-                out=last_norm[tiles][:],
-                in0=last_oT[tiles][:],
-                in1=last_rsum[tiles][:].unsqueeze(2).to_broadcast([P, n, P]),
-                op=ALU.mult,
+        def last_spread(tiles):
+            last_spread_ps[tiles] = psum_s.tile(
+                [P, len(tiles) * P], F32, name="last_spread_ps", tag="s_ps"
             )
-
-        def last_turn_back(tiles):
-            last_back[tiles] = psum_s.tile([P, len(tiles) * P], F32, name="last_back", tag="s_ps")
             for l in range(len(tiles)):
                 nc.tensor.transpose(
-                    last_back[tiles][:, l * P : (l + 1) * P], last_norm[tiles][:, l, :], ident[:]
+                    last_spread_ps[tiles][:, l * P : (l + 1) * P],
+                    last_rsum[tiles][:, l : l + 1].to_broadcast([P, P]),
+                    ident[:],
                 )
+
+        def last_scale(tiles):
+            h = LAST % HEADS
+            last_gain[tiles] = tail.tile([P, len(tiles) * P], F32, name="last_gain%d" % tiles[0])
+            nc.scalar.activation(
+                out=last_gain[tiles][:],
+                in_=last_spread_ps[tiles][:],
+                func=ACT.Copy,
+                scale=bn_scale[:, h : h + 1],
+            )
+
+        def last_attend(tiles):
+            last_o[tiles] = psum_s.tile([P, len(tiles) * P], F32, name="last_o", tag="s_ps")
+            nc.tensor.matmul_mx(
+                out=last_o[tiles][:],
+                lhsT=v_codes[LAST][:].bitcast(FP8X4),
+                lhsT_scale=v_scales[LAST][:],
+                rhs=last_codes[tiles][:].bitcast(FP8X4),
+                rhs_scale=last_scales[tiles][:],
+                start=True,
+                stop=True,
+            )
+
+        def last_multiply(tiles):
+            last_z[tiles] = tail.tile([P, len(tiles) * P], F32, name="last_z%d" % tiles[0])
+            nc.vector.tensor_tensor(
+                out=last_z[tiles][:], in0=last_o[tiles][:], in1=last_gain[tiles][:], op=ALU.mult
+            )
 
         def last_finish(tiles):
             b, h = divmod(LAST, HEADS)
             y_part = tail.tile([P, len(tiles) * P], F32, name="y_part%d" % tiles[0])
             nc.scalar.activation(
                 out=y_part[:],
-                in_=last_back[tiles][:],
+                in_=last_z[tiles][:],
                 func=ACT.Relu,
                 bias=bn_shift[:, h : h + 1],
-                scale=bn_scale[:, h : h + 1],
+                scale=1.0,
             )
             nc.sync.dma_start(
                 out=out[b, h * P : (h + 1) * P, tiles[0] * P : (tiles[-1] + 1) * P], in_=y_part[:]
@@ -489,6 +509,7 @@ def tile_bottleneck_transformer_pa_kernel(
         for i in range(LAST):
             g = i * NT
             scores(g + 4)
+            invert_pair(i - 2)
             rowmax(g + 2)
             exponent(g)
             if i == 0:
@@ -512,7 +533,6 @@ def tile_bottleneck_transformer_pa_kernel(
             rowmax(g + 4)
             turn(i, 0)
             exponent(g + 2)
-            invert(i - 1)
             quantise_e(i - 1)
             quantise_v(i - 1)
             finish(i - 2)
@@ -537,31 +557,35 @@ def tile_bottleneck_transformer_pa_kernel(
         exponent(g + 1)
         turn_back(LAST - 2)
         gather(LAST - 1, 1)
-        add_bias(LAST - 1)
-        project(LAST)
         last_turn(first)
+        add_bias(LAST - 1)
+        last_invert(first)
+        last_spread(first)
         exponent(g + 2)
         invert(LAST - 1)
         quantise_e(LAST - 1)
         quantise_v(LAST - 1)
         finish(LAST - 2)
+        project(LAST)
         exponent(g + 3)
         last_gather(first)
+        last_scale(first)
         attend(LAST - 1)
         add_bias(LAST)
-        quantise_v(LAST)
-        normalise(LAST - 1)
-        last_quantise(first)
+        last_invert(second)
         last_turn(second)
+        last_spread(second)
+        normalise(LAST - 1)
+        quantise_v(LAST)
+        last_quantise(first)
         last_gather(second)
+        last_scale(second)
         turn_back(LAST - 1)
         last_attend(first)
         last_quantise(second)
-        last_normalise(first)
+        last_multiply(first)
         finish(LAST - 1)
         last_attend(second)
-        last_normalise(second)
-        last_turn_back(first)
+        last_multiply(second)
         last_finish(first)
-        last_turn_back(second)
         last_finish(second)

@@ -360,6 +360,8 @@ def tile_bottleneck_transformer_pa_kernel(
             )
 
         bias_sb = consts.tile([P, N], F32, name="bias_sb")
+        minus_half = consts.tile([P, HEADS], F32, name="minus_half")
+        nc.gpsimd.memset(minus_half[:], -0.5)
         bn_scale = consts.tile([P, HEADS], F32, name="bn_scale")
         bn_shift = consts.tile([P, HEADS], F32, name="bn_shift")
 
@@ -379,8 +381,6 @@ def tile_bottleneck_transformer_pa_kernel(
             var = par_sb[:, 3 * HEADS : 4 * HEADS]
             rstd = consts.tile([P, HEADS], F32, name="rstd")
             scaled_mean = consts.tile([P, HEADS], F32, name="scaled_mean")
-            minus_half = consts.tile([P, HEADS], F32, name="minus_half")
-            nc.gpsimd.memset(minus_half[:], -0.5)
             nc.gpsimd.tensor_scalar_add(out=rstd[:], in0=var, scalar1=EPS)
             nc.gpsimd.tensor_tensor(out=rstd[:], in0=rstd[:], in1=minus_half[:], op=ALU.pow)
             nc.gpsimd.tensor_tensor(out=bn_scale[:], in0=gain, in1=rstd[:], op=ALU.mult)
@@ -502,6 +502,7 @@ def tile_bottleneck_transformer_pa_kernel(
         scores(0)
         scores(1)
         spread_bias()
+        spread_small_vectors()
         scores(2)
         scores(3)
         rowmax(0)
@@ -513,7 +514,6 @@ def tile_bottleneck_transformer_pa_kernel(
             rowmax(g + 2)
             exponent(g)
             if i == 0:
-                spread_small_vectors()
                 turn_weights()
             normalise(i - 2)
             turn(i - 1, 1)

@@ -373,16 +373,22 @@ def tile_bottleneck_transformer_pa_kernel(
         def spread_small_vectors():
             par_ps = psum_o.tile([P, P], BF16, name="par_ps", tag="shared")
             nc.tensor.transpose(par_ps[:], par_rows[:], ident_bf[:])
-            par_sb = consts.tile([P, 4 * HEADS], F32, name="par_sb")
-            nc.scalar.copy(out=par_sb[:], in_=par_ps[:, 0 : 4 * HEADS])
+            var_eps = consts.tile([P, HEADS], F32, name="var_eps")
+            nc.scalar.activation(
+                out=var_eps[:],
+                in_=par_ps[:, 3 * HEADS : 4 * HEADS],
+                func=ACT.Copy,
+                bias=EPS,
+                scale=1.0,
+            )
+            par_sb = consts.tile([P, 3 * HEADS], F32, name="par_sb")
+            nc.scalar.copy(out=par_sb[:], in_=par_ps[:, 0 : 3 * HEADS])
             gain = par_sb[:, 0 * HEADS : 1 * HEADS]
             shift = par_sb[:, 1 * HEADS : 2 * HEADS]
             mean = par_sb[:, 2 * HEADS : 3 * HEADS]
-            var = par_sb[:, 3 * HEADS : 4 * HEADS]
             rstd = consts.tile([P, HEADS], F32, name="rstd")
             scaled_mean = consts.tile([P, HEADS], F32, name="scaled_mean")
-            nc.gpsimd.tensor_scalar_add(out=rstd[:], in0=var, scalar1=EPS)
-            nc.gpsimd.tensor_tensor(out=rstd[:], in0=rstd[:], in1=minus_half[:], op=ALU.pow)
+            nc.gpsimd.tensor_tensor(out=rstd[:], in0=var_eps[:], in1=minus_half[:], op=ALU.pow)
             nc.gpsimd.tensor_tensor(out=bn_scale[:], in0=gain, in1=rstd[:], op=ALU.mult)
             nc.gpsimd.tensor_tensor(out=scaled_mean[:], in0=mean, in1=bn_scale[:], op=ALU.mult)
             nc.gpsimd.tensor_tensor(
@@ -500,9 +506,9 @@ def tile_bottleneck_transformer_pa_kernel(
         for r in range(WARM_MATMULS):
             nc.tensor.matmul(out=warm_ps[:], lhsT=zeros[:], rhs=zeros[:], start=True, stop=True)
         scores(0)
+        spread_small_vectors()
         scores(1)
         spread_bias()
-        spread_small_vectors()
         scores(2)
         scores(3)
         rowmax(0)

from contextlib import ExitStack

import concourse.masks as masks
import concourse.mybir as mybir

F32 = mybir.dt.float32
BF16 = mybir.dt.bfloat16
U32 = mybir.dt.uint32
U8 = mybir.dt.uint8
FP8X4 = mybir.dt.float8_e4m3fn_x4
ALU = mybir.AluOpType
ACT = mybir.ActivationFunctionType

P = 128
PACK = 4
B = 2
HEADS = 4
ROUNDS = B * HEADS
N = 512
LAST = ROUNDS - 1
NT = N // P
TILES = ROUNDS * NT
HALVES = 2
EPS = 1e-5
WARM_MATMULS = 16

FLOPS = 2 * B * N * N * N + 2 * (2 * ROUNDS * N * N * P) + 2 * ROUNDS * P * N * N


def tile_bottleneck_transformer_pa_kernel(
    tc, h1, v_w, v_b, q, k, pos, bn2_g, bn2_b, bn2_m, bn2_v, out
):
    nc = tc.nc
    with ExitStack() as ctx:
        consts = ctx.enter_context(tc.tile_pool(name="consts", bufs=1))
        inputs = ctx.enter_context(tc.tile_pool(name="inputs", bufs=1))
        operands = ctx.enter_context(tc.tile_pool(name="operands", bufs=1))
        e_pool = ctx.enter_context(tc.tile_pool(name="e_pool", bufs=6))
        stats = ctx.enter_context(tc.tile_pool(name="stats", bufs=3))
        work = ctx.enter_context(tc.tile_pool(name="work", bufs=2))
        results = ctx.enter_context(tc.tile_pool(name="results", bufs=3))
        tail = ctx.enter_context(tc.tile_pool(name="tail", bufs=1))
        psum_s = ctx.enter_context(tc.psum_pool(name="psum_s", bufs=5))
        psum_t = ctx.enter_context(tc.psum_pool(name="psum_t", bufs=1))
        psum_o = ctx.enter_context(tc.psum_pool(name="psum_o", bufs=2))

        zeros = consts.tile([P, P], BF16, name="zeros")
        nc.vector.memset(zeros[:], 0.0)
        par_rows = consts.tile([P, P], BF16, name="par_rows")
        nc.vector.memset(par_rows[:], 0.0)
        vb_row = consts.tile([P, N], BF16, name="vb_row")
        nc.vector.memset(vb_row[:], 0.0)
        ones_bf = consts.tile([P, P], BF16, name="ones_bf")
        nc.vector.memset(ones_bf[:], 1.0)
        ident = consts.tile([P, P], F32, name="ident")
        masks.make_identity(nc, ident[:])
        for r, vec in enumerate((bn2_g, bn2_b, bn2_m, bn2_v)):
            nc.scalar.dma_start(
                out=par_rows[r * HEADS : (r + 1) * HEADS, :],
                in_=vec.rearrange("(h d) -> h d", d=P),
            )
        ident_bf = consts.tile([P, P], BF16, name="ident_bf")
        masks.make_identity(nc, ident_bf[:])

        q_sb = [inputs.tile([P, N], BF16, name="q_sb%d" % i) for i in range(ROUNDS)]
        k_sb = [inputs.tile([P, N], BF16, name="k_sb%d" % i) for i in range(ROUNDS)]
        pos_sb = [inputs.tile([P, N], BF16, name="pos_sb%d" % h) for h in range(HEADS)]
        h_raw = [inputs.tile([P, PACK, N], BF16, name="h_raw%d" % b) for b in range(B)]
        w_raw = inputs.tile([P, NT, N], BF16, name="w_raw")

        def load_head(i):
            b, h = divmod(i, HEADS)
            channels = slice(h * P, (h + 1) * P)
            nc.sync.dma_start(out=q_sb[i][:], in_=q[b, channels, :])
            nc.sync.dma_start(out=k_sb[i][:], in_=k[b, channels, :])
            if b == 0:
                nc.sync.dma_start(out=pos_sb[h][:], in_=pos[h])

        def load_batch(b):
            nc.sync.dma_start(out=h_raw[b][:], in_=h1[b].rearrange("(p t) m -> p t m", t=PACK))

        load_head(0)
        nc.sync.dma_start(out=vb_row[0:1, :], in_=v_b.rearrange("(a o) -> a o", a=1))
        nc.sync.dma_start(out=w_raw[:], in_=v_w.rearrange("(a o) c -> o a c", o=P))
        load_head(1)
        load_batch(0)
        for i in range(2, HEADS):
            load_head(i)
        load_batch(1)
        for i in range(HEADS, ROUNDS):
            load_head(i)

        s_ps = {}
        negmax = {}
        esum = {}
        esum_pair = {}
        e_sb = {}
        eT_ps = {}
        e_grouped = {}
        e_codes = {}
        e_scales = {}
        vT_ps = {}
        v_grouped = {}
        v_codes = {}
        v_scales = {}
        rsum = {}
        oT_ps = {}
        oT_sb = {}
        o_ps = {}
        h_codes = {}
        h_scales = {}

        def scores(g):
            if g >= TILES:
                return
            i, nt = divmod(g, NT)
            rows = slice(nt * P, (nt + 1) * P)
            s_ps[g] = psum_s.tile([P, N], F32, name="s_ps")
            nc.tensor.matmul(
                out=s_ps[g][:], lhsT=q_sb[i][:, rows], rhs=k_sb[i][:], start=True, stop=False
            )
            nc.tensor.matmul(
                out=s_ps[g][:],
                lhsT=pos_sb[i % HEADS][:, rows],
                rhs=q_sb[i][:],
                start=False,
                stop=True,
            )

        def rowmax(g):
            if g >= TILES:
                return
            i, nt = divmod(g, NT)
            if nt == 0:
                negmax[i] = stats.tile([P, NT], F32, name="negmax")
            nc.vector.reduce_max(
                out=negmax[i][:, nt : nt + 1],
                in_=s_ps[g][:],
                axis=mybir.AxisListType.X,
                negate=True,
            )

        def exponent(g):
            if g >= TILES:
                return
            i, nt = divmod(g, NT)
            if nt == 0 and i % 2 == 0:
                sums = stats.tile([P, 2 * NT], F32, name="sums")
                esum[i] = sums[:, 0:NT]
                esum[i + 1] = sums[:, NT : 2 * NT]
                esum_pair[i] = sums
            e_sb[g] = e_pool.tile([P, N], BF16, name="e_sb")
            nc.scalar.activation(
                out=e_sb[g][:].rearrange("n (u p e) -> n u p e", u=2, e=2),
                in_=s_ps[g][:].rearrange("n (u e p) -> n u p e", u=2, e=2),
                func=ACT.Exp,
                bias=negmax[i][:, nt : nt + 1],
                scale=1.0,
                accum_out=esum[i][:, nt : nt + 1],
            )

        def turn(i, half):
            if not 0 <= i < ROUNDS - 1:
                return
            eT_ps[i, half] = psum_t.tile([P, HALVES, 2, P], F32, name="eT_ps", tag="turned")
            for l in range(HALVES):
                words = e_sb[i * NT + half * HALVES + l][:].bitcast(F32)
                for u in range(2):
                    nc.tensor.transpose(
                        eT_ps[i, half][:, l, u, :], words[:, u * P : (u + 1) * P], ident[:]
                    )

        def gather(i, half):
            if not 0 <= i < ROUNDS - 1:
                return
            if half == 0:
                e_grouped[i] = work.tile([P, N * PACK], BF16, name="e_grouped", align_bytes=64)
            words = e_grouped[i][:].bitcast(F32).rearrange(
                "p (c l n u) -> p c l n u", c=HALVES, l=HALVES, u=2
            )
            nc.scalar.copy(
                out=words[:, half], in_=eT_ps[i, half][:].rearrange("p l u n -> p l n u")
            )

        def quantise_e(i):
            if not 0 <= i < ROUNDS - 1:
                return
            e_codes[i] = work.tile([P, N], U32, name="e_codes", align_bytes=64)
            e_scales[i] = work.tile([P, N], U8, name="e_scales", align_bytes=64)
            nc.vector.quantize_mx(
                out=e_codes[i][:].bitcast(FP8X4), scales=e_scales[i][:], in_=e_grouped[i][:]
            )

        def project(i):
            if not 0 <= i < ROUNDS:
                return
            b, h = divmod(i, HEADS)
            channels = slice(h * P, (h + 1) * P)
            vT_ps[i] = psum_o.tile([P, PACK, P], F32, name="vT_ps", tag="shared")
            for t in range(PACK):
                positions = slice(t * P, (t + 1) * P)
                nc.tensor.matmul_mx(
                    out=vT_ps[i][:, t, :],
                    lhsT=h_codes[b][:, positions].bitcast(FP8X4),
                    lhsT_scale=h_scales[b][:, positions],
                    rhs=w_codes[:, channels].bitcast(FP8X4),
                    rhs_scale=w_scales[:, channels],
                    start=True,
                    stop=True,
                )

        def add_bias(i):
            if not 0 <= i < ROUNDS:
                return
            h = i % HEADS
            v_grouped[i] = work.tile([P, P, PACK], BF16, name="v_grouped", align_bytes=64)
            nc.vector.tensor_tensor(
                out=v_grouped[i][:],
                in0=vT_ps[i][:].rearrange("p t d -> p d t"),
                in1=bias_sb[:, h * P : (h + 1) * P].unsqueeze(2).to_broadcast([P, P, PACK]),
                op=ALU.add,
            )

        def quantise_v(i):
            if not 0 <= i < ROUNDS:
                return
            v_codes[i] = work.tile([P, P], U32, name="v_codes", align_bytes=64)
            v_scales[i] = work.tile([P, P], U8, name="v_scales", align_bytes=64)
            nc.vector.quantize_mx(
                out=v_codes[i][:].bitcast(FP8X4),
                scales=v_scales[i][:],
                in_=v_grouped[i][:].rearrange("p d t -> p (d t)"),
            )

        def attend(i):
            if not 0 <= i < ROUNDS - 1:
                return
            oT_ps[i] = psum_o.tile([P, NT, P], F32, name="oT_ps", tag="shared")
            for nt in range(NT):
                rows = slice(nt * P, (nt + 1) * P)
                nc.tensor.matmul_mx(
                    out=oT_ps[i][:, nt, :],
                    lhsT=e_codes[i][:, rows].bitcast(FP8X4),
                    lhsT_scale=e_scales[i][:, rows],
                    rhs=v_codes[i][:].bitcast(FP8X4),
                    rhs_scale=v_scales[i][:],
                    start=True,
                    stop=True,
                )

        def invert_pair(i):
            if not (i % 2 == 0 and 0 <= i < LAST - 1):
                return
            inverse = stats.tile([P, 2 * NT], F32, name="inverse")
            nc.vector.reciprocal(out=inverse[:], in_=esum_pair[i][:])
            rsum[i] = inverse[:, 0:NT]
            rsum[i + 1] = inverse[:, NT : 2 * NT]

        def invert(i):
            inverse_one = stats.tile([P, NT], F32, name="inverse_one")
            nc.vector.reciprocal(out=inverse_one[:], in_=esum[i])
            rsum[i] = inverse_one[:]

        def normalise(i):
            if not 0 <= i < LAST:
                return
            oT_sb[i] = work.tile([P, NT, P], F32, name="oT_sb")
            if i < 2:
                for nt in range(NT):
                    nc.scalar.activation(
                        out=oT_sb[i][:, nt, :],
                        in_=oT_ps[i][:, nt, :],
                        func=ACT.Copy,
                        scale=rsum[i][:, nt : nt + 1],
                    )
            else:
                nc.vector.tensor_tensor(
                    out=oT_sb[i][:],
                    in0=oT_ps[i][:],
                    in1=rsum[i].unsqueeze(2).to_broadcast([P, NT, P]),
                    op=ALU.mult,
                )

        def turn_back(i):
            if not 0 <= i < ROUNDS - 1:
                return
            o_ps[i] = psum_o.tile([P, N], F32, name="o_ps", tag="shared")
            for nt in range(NT):
                nc.tensor.transpose(
                    o_ps[i][:, nt * P : (nt + 1) * P], oT_sb[i][:, nt, :], ident[:]
                )

        def finish(i):
            if not 0 <= i < ROUNDS - 1:
                return
            b, h = divmod(i, HEADS)
            y_sb = results.tile([P, N], F32, name="y_sb")
            nc.scalar.activation(
                out=y_sb[:],
                in_=o_ps[i][:],
                func=ACT.Relu,
                bias=bn_shift[:, h : h + 1],
                scale=bn_scale[:, h : h + 1],
            )
            nc.sync.dma_start(out=out[b, h * P : (h + 1) * P, :], in_=y_sb[:])

        h_grouped = {}
        for b in range(B):
            h_grouped[b] = operands.tile([P, N, PACK], BF16, name="h_grouped%d" % b, align_bytes=64)
            h_codes[b] = operands.tile([P, N], U32, name="h_codes%d" % b, align_bytes=64)
            h_scales[b] = operands.tile([P, N], U8, name="h_scales%d" % b, align_bytes=64)

        def regroup(b, c):
            positions = slice(c * N // HALVES, (c + 1) * N // HALVES)
            nc.vector.tensor_copy(
                out=h_grouped[b][:, positions, :].rearrange("p (c i) t -> p c t i", i=4),
                in_=h_raw[b][:, :, positions].rearrange("p t (c i) -> p c t i", i=4),
            )

        def quantise_h(b):
            nc.vector.quantize_mx(
                out=h_codes[b][:].bitcast(FP8X4),
                scales=h_scales[b][:],
                in_=h_grouped[b][:].rearrange("p m t -> p (m t)"),
            )

        def prepare(i, step):
            if (i, step) in ((0, 2), (2, 1)):
                regroup(i // 2, 0)
            if (i, step) in ((0, 3), (2, 3)):
                regroup(i // 2, 1)
            if (i, step) in ((1, 0), (3, 1)):
                quantise_h(i // 2)

        w_grouped = operands.tile([P, N * PACK], BF16, name="w_grouped", align_bytes=64)
        w_codes = operands.tile([P, N], U32, name="w_codes", align_bytes=64)
        w_scales = operands.tile([P, N], U8, name="w_scales", align_bytes=64)

        wT_ps = {}

        def turn_weights():
            for c in range(HALVES):
                wT_ps[c] = psum_o.tile([P, HALVES, 2, P], F32, name="wT_ps", tag="shared")
                for l in range(HALVES):
                    words = (
                        w_raw[:, c * HALVES + l, :].bitcast(F32).rearrange("o (p u) -> o u p", u=2)
                    )
                    for u in range(2):
                        nc.tensor.transpose(wT_ps[c][:, l, u, :], words[:, u, :], ident[:])

        def gather_weights(c):
            w_words = w_grouped[:].bitcast(F32).rearrange(
                "p (c l o u) -> p c l o u", c=HALVES, l=HALVES, u=2
            )
            nc.scalar.copy(out=w_words[:, c], in_=wT_ps[c][:].rearrange("p l u o -> p l o u"))

        def quantise_weights():
            nc.vector.quantize_mx(
                out=w_codes[:].bitcast(FP8X4), scales=w_scales[:], in_=w_grouped[:]
            )

        bias_sb = consts.tile([P, N], F32, name="bias_sb")
        minus_half = consts.tile([P, HEADS], F32, name="minus_half")
        nc.gpsimd.memset(minus_half[:], -0.5)
        bn_scale = consts.tile([P, HEADS], F32, name="bn_scale")
        bn_shift = consts.tile([P, HEADS], F32, name="bn_shift")

        def spread_bias():
            bias_ps = psum_o.tile([P, N], F32, name="bias_ps", tag="shared")
            nc.tensor.matmul(out=bias_ps[:], lhsT=ones_bf[:], rhs=vb_row[:], start=True, stop=True)
            nc.scalar.copy(out=bias_sb[:], in_=bias_ps[:])

        def spread_small_vectors():
            par_ps = psum_o.tile([P, P], BF16, name="par_ps", tag="shared")
            nc.tensor.transpose(par_ps[:], par_rows[:], ident_bf[:])
            var_eps = consts.tile([P, HEADS], F32, name="var_eps")
            nc.scalar.activation(
                out=var_eps[:],
                in_=par_ps[:, 3 * HEADS : 4 * HEADS],
                func=ACT.Copy,
                bias=EPS,
                scale=1.0,
            )
            par_sb = consts.tile([P, 3 * HEADS], F32, name="par_sb")
            nc.scalar.copy(out=par_sb[:], in_=par_ps[:, 0 : 3 * HEADS])
            gain = par_sb[:, 0 * HEADS : 1 * HEADS]
            shift = par_sb[:, 1 * HEADS : 2 * HEADS]
            mean = par_sb[:, 2 * HEADS : 3 * HEADS]
            rstd = consts.tile([P, HEADS], F32, name="rstd")
            scaled_mean = consts.tile([P, HEADS], F32, name="scaled_mean")
            nc.gpsimd.tensor_tensor(out=rstd[:], in0=var_eps[:], in1=minus_half[:], op=ALU.pow)
            nc.gpsimd.tensor_tensor(out=bn_scale[:], in0=gain, in1=rstd[:], op=ALU.mult)
            nc.gpsimd.tensor_tensor(out=scaled_mean[:], in0=mean, in1=bn_scale[:], op=ALU.mult)
            nc.gpsimd.tensor_tensor(
                out=bn_shift[:], in0=shift, in1=scaled_mean[:], op=ALU.subtract
            )

        last_turned = {}
        last_grouped = {}
        last_codes = {}
        last_scales = {}
        last_rsum = {}
        last_spread_ps = {}
        last_gain = {}
        last_o = {}
        last_z = {}

        def last_turn(tiles):
            last_turned[tiles] = psum_s.tile([P, len(tiles), 2, P], F32, name="last_turned", tag="s_ps")
            for l, nt in enumerate(tiles):
                words = e_sb[LAST * NT + nt][:].bitcast(F32)
                for u in range(2):
                    nc.tensor.transpose(
                        last_turned[tiles][:, l, u, :], words[:, u * P : (u + 1) * P], ident[:]
                    )

        def last_gather(tiles):
            n = len(tiles)
            last_grouped[tiles] = tail.tile(
                [P, n * P * PACK], BF16, name="last_grouped%d" % tiles[0], align_bytes=64
            )
            nc.scalar.copy(
                out=last_grouped[tiles][:].bitcast(F32).rearrange("p (l n u) -> p l n u", l=n, u=2),
                in_=last_turned[tiles][:].rearrange("p l u n -> p l n u"),
            )

        def last_quantise(tiles):
            n = len(tiles)
            last_codes[tiles] = tail.tile([P, n * P], U32, name="last_codes%d" % tiles[0], align_bytes=64)
            last_scales[tiles] = tail.tile([P, n * P], U8, name="last_scales%d" % tiles[0], align_bytes=64)
            nc.vector.quantize_mx(
                out=last_codes[tiles][:].bitcast(FP8X4),
                scales=last_scales[tiles][:],
                in_=last_grouped[tiles][:],
            )

        def last_invert(tiles):
            last_rsum[tiles] = tail.tile([P, len(tiles)], F32, name="last_rsum%d" % tiles[0])
            nc.vector.reciprocal(
                out=last_rsum[tiles][:], in_=esum[LAST][:, tiles[0] : tiles[-1] + 1]
            )

        def last_spread(tiles):
            last_spread_ps[tiles] = psum_s.tile(
                [P, len(tiles) * P], F32, name="last_spread_ps", tag="s_ps"
            )
            for l in range(len(tiles)):
                nc.tensor.transpose(
                    last_spread_ps[tiles][:, l * P : (l + 1) * P],
                    last_rsum[tiles][:, l : l + 1].to_broadcast([P, P]),
                    ident[:],
                )

        def last_scale(tiles):
            h = LAST % HEADS
            last_gain[tiles] = tail.tile([P, len(tiles) * P], F32, name="last_gain%d" % tiles[0])
            nc.scalar.activation(
                out=last_gain[tiles][:],
                in_=last_spread_ps[tiles][:],
                func=ACT.Copy,
                scale=bn_scale[:, h : h + 1],
            )

        def last_attend(tiles):
            last_o[tiles] = psum_s.tile([P, len(tiles) * P], F32, name="last_o", tag="s_ps")
            nc.tensor.matmul_mx(
                out=last_o[tiles][:],
                lhsT=v_codes[LAST][:].bitcast(FP8X4),
                lhsT_scale=v_scales[LAST][:],
                rhs=last_codes[tiles][:].bitcast(FP8X4),
                rhs_scale=last_scales[tiles][:],
                start=True,
                stop=True,
            )

        def last_multiply(tiles):
            last_z[tiles] = tail.tile([P, len(tiles) * P], F32, name="last_z%d" % tiles[0])
            nc.vector.tensor_tensor(
                out=last_z[tiles][:], in0=last_o[tiles][:], in1=last_gain[tiles][:], op=ALU.mult
            )

        def last_finish(tiles):
            b, h = divmod(LAST, HEADS)
            y_part = tail.tile([P, len(tiles) * P], F32, name="y_part%d" % tiles[0])
            nc.scalar.activation(
                out=y_part[:],
                in_=last_z[tiles][:],
                func=ACT.Relu,
                bias=bn_shift[:, h : h + 1],
                scale=1.0,
            )
            nc.sync.dma_start(
                out=out[b, h * P : (h + 1) * P, tiles[0] * P : (tiles[-1] + 1) * P], in_=y_part[:]
            )

        ctx.enter_context(
            tc.manual_schedule(
                engines={
                    mybir.EngineType.PE,
                    mybir.EngineType.DVE,
                    mybir.EngineType.Activation,
                }
            )
        )
        warm_ps = psum_o.tile([P, P], F32, name="warm_ps", tag="shared")
        for r in range(WARM_MATMULS):
            nc.tensor.matmul(out=warm_ps[:], lhsT=zeros[:], rhs=zeros[:], start=True, stop=True)
        scores(0)
        spread_small_vectors()
        scores(1)
        spread_bias()
        scores(2)
        scores(3)
        rowmax(0)
        rowmax(1)
        for i in range(LAST):
            g = i * NT
            scores(g + 4)
            invert_pair(i - 2)
            rowmax(g + 2)
            exponent(g)
            if i == 0:
                turn_weights()
            normalise(i - 2)
            turn(i - 1, 1)
            prepare(i, 0)
            project(i - 1)
            scores(g + 5)
            rowmax(g + 3)
            exponent(g + 1)
            turn_back(i - 2)
            gather(i - 1, 1)
            if i == 0:
                gather_weights(0)
                gather_weights(1)
            add_bias(i - 1)
            prepare(i, 1)
            scores(g + 6)
            rowmax(g + 4)
            turn(i, 0)
            exponent(g + 2)
            quantise_e(i - 1)
            quantise_v(i - 1)
            finish(i - 2)
            prepare(i, 2)
            scores(g + 7)
            rowmax(g + 5)
            exponent(g + 3)
            gather(i, 0)
            if i == 0:
                quantise_weights()
            attend(i - 1)
            prepare(i, 3)

        first, second = (0, 1), (2, 3)
        g = LAST * NT
        rowmax(g + 2)
        exponent(g)
        normalise(LAST - 2)
        turn(LAST - 1, 1)
        project(LAST - 1)
        rowmax(g + 3)
        exponent(g + 1)
        turn_back(LAST - 2)
        gather(LAST - 1, 1)
        last_turn(first)
        add_bias(LAST - 1)
        last_invert(first)
        last_spread(first)
        exponent(g + 2)
        invert(LAST - 1)
        quantise_e(LAST - 1)
        quantise_v(LAST - 1)
        finish(LAST - 2)
        project(LAST)
        exponent(g + 3)
        last_gather(first)
        last_scale(first)
        attend(LAST - 1)
        add_bias(LAST)
        last_invert(second)
        last_turn(second)
        last_spread(second)
        normalise(LAST - 1)
        quantise_v(LAST)
        last_quantise(first)
        last_gather(second)
        last_scale(second)
        turn_back(LAST - 1)
        last_attend(first)
        last_quantise(second)
        last_multiply(first)
        finish(LAST - 1)
        last_attend(second)
        last_multiply(second)
        last_finish(first)
        last_finish(second)
